import numpy as np
import ml_dtypes


def mxq(x, axis, fmt="e4m3"):
    dtype, down = {"e4m3": (ml_dtypes.float8_e4m3fn, 7), "e5m2": (ml_dtypes.float8_e5m2, 14)}[fmt]
    v = np.moveaxis(np.asarray(x, np.float32).astype(ml_dtypes.bfloat16).astype(np.float64), axis, -1)
    blocks = v.reshape(v.shape[:-1] + (-1, 32))
    amax = np.abs(blocks).max(-1, keepdims=True)
    byte = np.maximum(np.where(amax > 0, np.frexp(amax)[1] - 1 + 127, 0) - down, 1)
    scale = np.exp2(byte - 127.0)
    codes = (blocks / scale).astype(np.float32).astype(dtype).astype(np.float64)
    return np.moveaxis((codes * scale).reshape(v.shape), -1, axis)


WIDE = False


def mx_kscale(k):
    if not WIDE:
        return np.ones(k)
    levels = np.array([10, -10, 5, -5, 0])
    a = np.random.permutation(np.resize(levels, k // 512 * 4)).reshape(k // 512, 4)
    idx = np.arange(k)
    return np.exp2(a[idx // 512, idx % 128 // 32])


BF16 = ml_dtypes.bfloat16


def bf(x):
    return np.asarray(x, np.float32).astype(BF16)


def f64(x):
    return np.asarray(x).astype(np.float64)


BS, CIN, COUT, OUT_DIM, BLK = 1024, 128, 512, 8, 4
D = OUT_DIM * BLK
K = CIN * BLK


def setup_inputs():
    s = mx_kscale(K)
    sd = np.tile(s.reshape(CIN, 1, BLK), (1, OUT_DIM, 1)).reshape(CIN, D)
    return {"x": bf(np.random.standard_normal((BS, CIN, D)) * sd),
            "weight": bf(np.random.standard_normal((COUT, CIN, D)) / sd)}


def reference(x, weight):
    bs, cin, d = x.shape
    cout = weight.shape[0]
    n = d // BLK
    xr = f64(x).reshape(bs, cin, n, BLK).transpose(2, 0, 1, 3).reshape(n, bs, cin * BLK)
    wr = f64(weight).reshape(cout, cin, n, BLK).transpose(2, 1, 3, 0).reshape(n, cin * BLK, cout)
    out = mxq(xr, 2, "e4m3") @ mxq(wr, 1, "e4m3")
    return out.transpose(1, 2, 0) / np.sqrt(cin)

@@ -1,0 +1,119 @@
+import math
+from contextlib import ExitStack
+
+import concourse.mybir as mybir
+from concourse.masks import make_identity
+
+FLOPS = 2 * 8 * 1024 * 512 * 512
+
+F32 = mybir.dt.float32
+BF16 = mybir.dt.bfloat16
+U32 = mybir.dt.uint32
+U8 = mybir.dt.uint8
+FP8X4 = mybir.dt.float8_e4m3fn_x4
+
+P = 128
+CIN = 128
+D = 32
+POS = 8
+WORDS = D // 2
+ROW = CIN * D
+BANK = 512
+W_TILES = 4
+X_TILES = 8
+INV = 1.0 / math.sqrt(CIN)
+
+
+def tile_nonoverlappinglocallyconnected1d_t_kernel(tc, x, weight, out):
+    nc = tc.nc
+    with ExitStack() as ctx:
+        const = ctx.enter_context(tc.tile_pool(name="const", bufs=1))
+        raws = ctx.enter_context(tc.tile_pool(name="raws", bufs=W_TILES + X_TILES))
+        stage = ctx.enter_context(tc.tile_pool(name="stage", bufs=3))
+        wkeep = ctx.enter_context(tc.tile_pool(name="wkeep", bufs=W_TILES))
+        xkeep = ctx.enter_context(tc.tile_pool(name="xkeep", bufs=3))
+        outs = ctx.enter_context(tc.tile_pool(name="outs", bufs=4))
+        psum = ctx.enter_context(tc.psum_pool(name="psum", bufs=8))
+        ctx.enter_context(tc.manual_schedule())
+
+        ident = const.tile([P, P], F32)
+        make_identity(nc, ident[:])
+
+        raw_tiles = []
+        for r in range(W_TILES + X_TILES):
+            raw = raws.tile([P, ROW], BF16, tag="raw")
+            if r < W_TILES:
+                rows = weight[r * P:(r + 1) * P, :, :]
+            else:
+                rows = x[(r - W_TILES) * P:(r - W_TILES + 1) * P, :, :]
+            nc.sync.dma_start(out=raw[:], in_=rows.rearrange("b i d -> b (i d)"))
+            raw_tiles.append(raw)
+
+        grouped_tiles = {}
+        code_tiles = {}
+
+        def flip(r):
+            words = raw_tiles[r][:].bitcast(F32).rearrange("p (i w) -> p w i", w=WORDS)
+            grouped = stage.tile([P, POS * P * 4], BF16, tag="grouped", align_bytes=64)
+            g32 = grouped[:].bitcast(F32)
+            for j in range(4):
+                bank = psum.tile([P, BANK], F32, tag="bank")
+                for wl in range(4):
+                    nc.tensor.transpose(bank[:, wl * P:(wl + 1) * P], words[:, 4 * j + wl, :], ident[:])
+                src = bank[:].rearrange("p (n u b) -> p n b u", n=2, u=2)
+                dst = g32[:, j * BANK:(j + 1) * BANK].rearrange("p (n b u) -> p n b u", n=2, u=2)
+                if j < 3:
+                    nc.scalar.copy(out=dst, in_=src)
+                else:
+                    nc.vector.tensor_copy(out=dst, in_=src)
+            grouped_tiles[r] = grouped
+
+        def quant(r):
+            pool = wkeep if r < W_TILES else xkeep
+            codes = pool.tile([P, POS * P], U32, tag="codes", align_bytes=64)
+            scales = pool.tile([P, POS * P], U8, tag="scales", align_bytes=64)
+            grouped = grouped_tiles[r]
+            for h in range(2):
+                nc.vector.quantize_mx(
+                    out=codes[:, h * 512:(h + 1) * 512].bitcast(FP8X4),
+                    scales=scales[:, h * 512:(h + 1) * 512],
+                    in_=grouped[:, h * 2048:(h + 1) * 2048],
+                )
+            code_tiles[r] = (codes, scales)
+
+        def mult(bt):
+            xc, xs = code_tiles[W_TILES + bt]
+            res = outs.tile([P, 512, POS], F32, tag="res")
+            for h in range(2):
+                for c in range(W_TILES):
+                    wc, ws = code_tiles[c]
+                    bank = psum.tile([P, BANK], F32, tag="bank")
+                    for nl in range(4):
+                        n = 4 * h + nl
+                        cols = slice(n * P, (n + 1) * P)
+                        nc.tensor.matmul_mx(
+                            out=bank[:, nl * P:(nl + 1) * P],
+                            lhsT=xc[:, cols].bitcast(FP8X4),
+                            lhsT_scale=xs[:, cols],
+                            rhs=wc[:, cols].bitcast(FP8X4),
+                            rhs_scale=ws[:, cols],
+                            start=True,
+                            stop=True,
+                        )
+                    src = bank[:].rearrange("p (n o) -> p o n", n=4)
+                    dst = res[:, c * P:(c + 1) * P, 4 * h:4 * h + 4]
+                    if c % 2 == 0:
+                        nc.vector.tensor_scalar(out=dst, in0=src, scalar1=INV, scalar2=None, op0=mybir.AluOpType.mult)
+                    else:
+                        nc.scalar.activation(out=dst, in_=src, func=mybir.ActivationFunctionType.Copy, scale=INV)
+            nc.sync.dma_start(out=out[bt * P:(bt + 1) * P, :, :], in_=res[:])
+
+        flip(0)
+        for r in range(1, W_TILES + 1):
+            flip(r)
+            quant(r - 1)
+        for bt in range(X_TILES):
+            quant(W_TILES + bt)
+            if bt + 1 < X_TILES:
+                flip(W_TILES + bt + 1)
+            mult(bt)

@@ -84,8 +84,13 @@ def tile_nonoverlappinglocallyconnected1d_t_kernel(tc, x, weight, out):
         def mult(bt):
             xc, xs = code_tiles[W_TILES + bt]
             res = outs.tile([P, 512, POS], F32, tag="res")
-            for h in range(2):
-                for c in range(W_TILES):
+            last = bt == X_TILES - 1
+            if last:
+                order = [(h, c) for c in range(W_TILES) for h in range(2)]
+            else:
+                order = [(h, c) for h in range(2) for c in range(W_TILES)]
+            for h, c in order:
+                if True:
                     wc, ws = code_tiles[c]
                     bank = psum.tile([P, BANK], F32, tag="bank")
                     for nl in range(4):
@@ -106,7 +111,10 @@ def tile_nonoverlappinglocallyconnected1d_t_kernel(tc, x, weight, out):
                         nc.vector.tensor_scalar(out=dst, in0=src, scalar1=INV, scalar2=None, op0=mybir.AluOpType.mult)
                     else:
                         nc.scalar.activation(out=dst, in_=src, func=mybir.ActivationFunctionType.Copy, scale=INV)
-            nc.sync.dma_start(out=out[bt * P:(bt + 1) * P, :, :], in_=res[:])
+                    if last and h == 1:
+                        nc.sync.dma_start(out=out[bt * P:(bt + 1) * P, c * P:(c + 1) * P, :], in_=res[:, c * P:(c + 1) * P, :])
+            if not last:
+                nc.sync.dma_start(out=out[bt * P:(bt + 1) * P, :, :], in_=res[:])
 
         flip(0)
         for r in range(1, W_TILES + 1):

@@ -41,7 +41,7 @@ def tile_nonoverlappinglocallyconnected1d_t_kernel(tc, x, weight, out):
 
         raw_tiles = []
         for r in range(W_TILES + X_TILES):
-            raw = raws.tile([P, ROW], BF16, tag="raw")
+            raw = raws.tile([P, ROW], BF16, tag="raw", align_bytes=256)
             if r < W_TILES:
                 rows = weight[r * P:(r + 1) * P, :, :]
             else:
@@ -83,7 +83,7 @@ def tile_nonoverlappinglocallyconnected1d_t_kernel(tc, x, weight, out):
 
         def mult(bt):
             xc, xs = code_tiles[W_TILES + bt]
-            res = outs.tile([P, 512, POS], F32, tag="res")
+            res = outs.tile([P, 512, POS], F32, tag="res", align_bytes=256)
             last = bt == X_TILES - 1
             if last:
                 order = [(h, c) for c in range(W_TILES) for h in range(2)]

@@ -84,13 +84,8 @@ def tile_nonoverlappinglocallyconnected1d_t_kernel(tc, x, weight, out):
         def mult(bt):
             xc, xs = code_tiles[W_TILES + bt]
             res = outs.tile([P, 512, POS], F32, tag="res", align_bytes=256)
-            last = bt == X_TILES - 1
-            if last:
-                order = [(h, c) for c in range(W_TILES) for h in range(2)]
-            else:
-                order = [(h, c) for h in range(2) for c in range(W_TILES)]
-            for h, c in order:
-                if True:
+            for h in range(2):
+                for c in range(W_TILES):
                     wc, ws = code_tiles[c]
                     bank = psum.tile([P, BANK], F32, tag="bank")
                     for nl in range(4):
@@ -111,10 +106,7 @@ def tile_nonoverlappinglocallyconnected1d_t_kernel(tc, x, weight, out):
                         nc.vector.tensor_scalar(out=dst, in0=src, scalar1=INV, scalar2=None, op0=mybir.AluOpType.mult)
                     else:
                         nc.scalar.activation(out=dst, in_=src, func=mybir.ActivationFunctionType.Copy, scale=INV)
-                    if last and h == 1:
-                        nc.sync.dma_start(out=out[bt * P:(bt + 1) * P, c * P:(c + 1) * P, :], in_=res[:, c * P:(c + 1) * P, :])
-            if not last:
-                nc.sync.dma_start(out=out[bt * P:(bt + 1) * P, :, :], in_=res[:])
+            nc.sync.dma_start(out=out[bt * P:(bt + 1) * P, :, :], in_=res[:])
 
         flip(0)
         for r in range(1, W_TILES + 1):

@@ -39,15 +39,15 @@ def tile_nonoverlappinglocallyconnected1d_t_kernel(tc, x, weight, out):
         ident = const.tile([P, P], F32)
         make_identity(nc, ident[:])
 
-        raw_tiles = []
-        for r in range(W_TILES + X_TILES):
+        raw_tiles = {}
+        for r in [0, W_TILES] + list(range(1, W_TILES)) + list(range(W_TILES + 1, W_TILES + X_TILES)):
             raw = raws.tile([P, ROW], BF16, tag="raw", align_bytes=256)
             if r < W_TILES:
                 rows = weight[r * P:(r + 1) * P, :, :]
             else:
                 rows = x[(r - W_TILES) * P:(r - W_TILES + 1) * P, :, :]
             nc.sync.dma_start(out=raw[:], in_=rows.rearrange("b i d -> b (i d)"))
-            raw_tiles.append(raw)
+            raw_tiles[r] = raw
 
         grouped_tiles = {}
         code_tiles = {}
@@ -81,39 +81,60 @@ def tile_nonoverlappinglocallyconnected1d_t_kernel(tc, x, weight, out):
                 )
             code_tiles[r] = (codes, scales)
 
-        def mult(bt):
+        def mult_part(bt, res, h, c, on_vector):
             xc, xs = code_tiles[W_TILES + bt]
-            res = outs.tile([P, 512, POS], F32, tag="res", align_bytes=256)
-            for h in range(2):
-                for c in range(W_TILES):
-                    wc, ws = code_tiles[c]
-                    bank = psum.tile([P, BANK], F32, tag="bank")
-                    for nl in range(4):
-                        n = 4 * h + nl
-                        cols = slice(n * P, (n + 1) * P)
-                        nc.tensor.matmul_mx(
-                            out=bank[:, nl * P:(nl + 1) * P],
-                            lhsT=xc[:, cols].bitcast(FP8X4),
-                            lhsT_scale=xs[:, cols],
-                            rhs=wc[:, cols].bitcast(FP8X4),
-                            rhs_scale=ws[:, cols],
-                            start=True,
-                            stop=True,
-                        )
-                    src = bank[:].rearrange("p (n o) -> p o n", n=4)
-                    dst = res[:, c * P:(c + 1) * P, 4 * h:4 * h + 4]
-                    if c % 2 == 0:
-                        nc.vector.tensor_scalar(out=dst, in0=src, scalar1=INV, scalar2=None, op0=mybir.AluOpType.mult)
-                    else:
-                        nc.scalar.activation(out=dst, in_=src, func=mybir.ActivationFunctionType.Copy, scale=INV)
+            wc, ws = code_tiles[c]
+            bank = psum.tile([P, BANK], F32, tag="bank")
+            for nl in range(4):
+                n = 4 * h + nl
+                cols = slice(n * P, (n + 1) * P)
+                nc.tensor.matmul_mx(
+                    out=bank[:, nl * P:(nl + 1) * P],
+                    lhsT=xc[:, cols].bitcast(FP8X4),
+                    lhsT_scale=xs[:, cols],
+                    rhs=wc[:, cols].bitcast(FP8X4),
+                    rhs_scale=ws[:, cols],
+                    start=True,
+                    stop=True,
+                )
+            src = bank[:].rearrange("p (n o) -> p o n", n=4)
+            dst = res[:, c * P:(c + 1) * P, 4 * h:4 * h + 4]
+            if on_vector:
+                nc.vector.tensor_scalar(out=dst, in0=src, scalar1=INV, scalar2=None, op0=mybir.AluOpType.mult)
+            else:
+                nc.scalar.activation(out=dst, in_=src, func=mybir.ActivationFunctionType.Copy, scale=INV)
+
+        def store(bt, res):
             nc.sync.dma_start(out=out[bt * P:(bt + 1) * P, :, :], in_=res[:])
 
+        res = outs.tile([P, 512, POS], F32, tag="res", align_bytes=256)
+
+        def first_products(c):
+            for h in range(2):
+                mult_part(0, res, h, c, on_vector=(h == 0))
+
         flip(0)
-        for r in range(1, W_TILES + 1):
-            flip(r)
-            quant(r - 1)
-        for bt in range(X_TILES):
+        flip(W_TILES)
+        quant(0)
+        flip(1)
+        quant(W_TILES)
+        flip(2)
+        quant(1)
+        first_products(0)
+        flip(3)
+        quant(2)
+        quant(3)
+        for c in range(1, W_TILES):
+            first_products(c)
+        store(0, res)
+
+        flip(W_TILES + 1)
+        for bt in range(1, X_TILES):
             quant(W_TILES + bt)
             if bt + 1 < X_TILES:
                 flip(W_TILES + bt + 1)
-            mult(bt)
+            res = outs.tile([P, 512, POS], F32, tag="res", align_bytes=256)
+            for h in range(2):
+                for c in range(W_TILES):
+                    mult_part(bt, res, h, c, on_vector=(c % 2 == 0))
+            store(bt, res)

import math
from contextlib import ExitStack

import concourse.mybir as mybir
from concourse.masks import make_identity

FLOPS = 2 * 8 * 1024 * 512 * 512

F32 = mybir.dt.float32
BF16 = mybir.dt.bfloat16
U32 = mybir.dt.uint32
U8 = mybir.dt.uint8
FP8X4 = mybir.dt.float8_e4m3fn_x4

P = 128
CIN = 128
D = 32
POS = 8
WORDS = D // 2
ROW = CIN * D
BANK = 512
W_TILES = 4
X_TILES = 8
INV = 1.0 / math.sqrt(CIN)


def tile_nonoverlappinglocallyconnected1d_t_kernel(tc, x, weight, out):
    nc = tc.nc
    with ExitStack() as ctx:
        const = ctx.enter_context(tc.tile_pool(name="const", bufs=1))
        raws = ctx.enter_context(tc.tile_pool(name="raws", bufs=W_TILES + X_TILES))
        stage = ctx.enter_context(tc.tile_pool(name="stage", bufs=3))
        wkeep = ctx.enter_context(tc.tile_pool(name="wkeep", bufs=W_TILES))
        xkeep = ctx.enter_context(tc.tile_pool(name="xkeep", bufs=3))
        outs = ctx.enter_context(tc.tile_pool(name="outs", bufs=4))
        psum = ctx.enter_context(tc.psum_pool(name="psum", bufs=8))
        ctx.enter_context(tc.manual_schedule())

        ident = const.tile([P, P], F32)
        make_identity(nc, ident[:])

        raw_tiles = {}
        for r in [0, W_TILES] + list(range(1, W_TILES)) + list(range(W_TILES + 1, W_TILES + X_TILES)):
            raw = raws.tile([P, ROW], BF16, tag="raw", align_bytes=256)
            if r < W_TILES:
                rows = weight[r * P:(r + 1) * P, :, :]
            else:
                rows = x[(r - W_TILES) * P:(r - W_TILES + 1) * P, :, :]
            nc.sync.dma_start(out=raw[:], in_=rows.rearrange("b i d -> b (i d)"))
            raw_tiles[r] = raw

        grouped_tiles = {}
        code_tiles = {}

        def flip(r):
            words = raw_tiles[r][:].bitcast(F32).rearrange("p (i w) -> p w i", w=WORDS)
            grouped = stage.tile([P, POS * P * 4], BF16, tag="grouped", align_bytes=64)
            g32 = grouped[:].bitcast(F32)
            for j in range(4):
                bank = psum.tile([P, BANK], F32, tag="bank")
                for wl in range(4):
                    nc.tensor.transpose(bank[:, wl * P:(wl + 1) * P], words[:, 4 * j + wl, :], ident[:])
                src = bank[:].rearrange("p (n u b) -> p n b u", n=2, u=2)
                dst = g32[:, j * BANK:(j + 1) * BANK].rearrange("p (n b u) -> p n b u", n=2, u=2)
                if j < 3:
                    nc.scalar.copy(out=dst, in_=src)
                else:
                    nc.vector.tensor_copy(out=dst, in_=src)
            grouped_tiles[r] = grouped

        def quant(r):
            pool = wkeep if r < W_TILES else xkeep
            codes = pool.tile([P, POS * P], U32, tag="codes", align_bytes=64)
            scales = pool.tile([P, POS * P], U8, tag="scales", align_bytes=64)
            grouped = grouped_tiles[r]
            for h in range(2):
                nc.vector.quantize_mx(
                    out=codes[:, h * 512:(h + 1) * 512].bitcast(FP8X4),
                    scales=scales[:, h * 512:(h + 1) * 512],
                    in_=grouped[:, h * 2048:(h + 1) * 2048],
                )
            code_tiles[r] = (codes, scales)

        def mult_part(bt, res, h, c, on_vector):
            xc, xs = code_tiles[W_TILES + bt]
            wc, ws = code_tiles[c]
            bank = psum.tile([P, BANK], F32, tag="bank")
            for nl in range(4):
                n = 4 * h + nl
                cols = slice(n * P, (n + 1) * P)
                nc.tensor.matmul_mx(
                    out=bank[:, nl * P:(nl + 1) * P],
                    lhsT=xc[:, cols].bitcast(FP8X4),
                    lhsT_scale=xs[:, cols],
                    rhs=wc[:, cols].bitcast(FP8X4),
                    rhs_scale=ws[:, cols],
                    start=True,
                    stop=True,
                )
            src = bank[:].rearrange("p (n o) -> p o n", n=4)
            dst = res[:, c * P:(c + 1) * P, 4 * h:4 * h + 4]
            if on_vector:
                nc.vector.tensor_scalar(out=dst, in0=src, scalar1=INV, scalar2=None, op0=mybir.AluOpType.mult)
            else:
                nc.scalar.activation(out=dst, in_=src, func=mybir.ActivationFunctionType.Copy, scale=INV)

        def store(bt, res):
            nc.sync.dma_start(out=out[bt * P:(bt + 1) * P, :, :], in_=res[:])

        res = outs.tile([P, 512, POS], F32, tag="res", align_bytes=256)

        def first_products(c):
            for h in range(2):
                mult_part(0, res, h, c, on_vector=(h == 0))

        flip(0)
        flip(W_TILES)
        quant(0)
        flip(1)
        quant(W_TILES)
        flip(2)
        quant(1)
        first_products(0)
        flip(3)
        quant(2)
        quant(3)
        for c in range(1, W_TILES):
            first_products(c)
        store(0, res)

        flip(W_TILES + 1)
        for bt in range(1, X_TILES):
            quant(W_TILES + bt)
            if bt + 1 < X_TILES:
                flip(W_TILES + bt + 1)
            res = outs.tile([P, 512, POS], F32, tag="res", align_bytes=256)
            for h in range(2):
                for c in range(W_TILES):
                    mult_part(bt, res, h, c, on_vector=(c % 2 == 0))
            store(bt, res)
